import numpy as np
import ml_dtypes


def mxq(x, axis, fmt="e4m3"):
    dtype, down = {"e4m3": (ml_dtypes.float8_e4m3fn, 7), "e5m2": (ml_dtypes.float8_e5m2, 14)}[fmt]
    v = np.moveaxis(np.asarray(x, np.float32).astype(ml_dtypes.bfloat16).astype(np.float64), axis, -1)
    blocks = v.reshape(v.shape[:-1] + (-1, 32))
    amax = np.abs(blocks).max(-1, keepdims=True)
    byte = np.maximum(np.where(amax > 0, np.frexp(amax)[1] - 1 + 127, 0) - down, 1)
    scale = np.exp2(byte - 127.0)
    codes = (blocks / scale).astype(np.float32).astype(dtype).astype(np.float64)
    return np.moveaxis((codes * scale).reshape(v.shape), -1, axis)


WIDE = False


def mx_kscale(k):
    if not WIDE:
        return np.ones(k)
    levels = np.array([10, -10, 5, -5, 0])
    a = np.random.permutation(np.resize(levels, k // 512 * 4)).reshape(k // 512, 4)
    idx = np.arange(k)
    return np.exp2(a[idx // 512, idx % 128 // 32])


BF16 = ml_dtypes.bfloat16


def bf(x):
    return np.asarray(x, np.float32).astype(BF16)


def f64(x):
    return np.asarray(x).astype(np.float64)


E2M1 = np.array([0.0, 0.5, 1.0, 1.5, 2.0, 3.0, 4.0, 6.0, -0.0, -0.5, -1.0, -1.5, -2.0, -3.0, -4.0, -6.0])


def pack_weight(w, fmt):
    k, n = w.shape
    w = f64(bf(w)).reshape(k // 32, 32, n)
    amax = np.abs(w).max(1)
    if fmt == "e4m3":
        byte = np.frexp(amax)[1] - 1 + 127 - 7
    else:
        mant, ex = np.frexp(amax / 6.0)
        byte = np.where(mant > 0.5, ex, ex - 1) + 127
    byte = np.clip(np.where(amax > 0, byte, 1), 1, 254)
    scaled = (w * np.exp2(127.0 - byte)[:, None, :]).reshape(k, n).astype(np.float32)
    by_word = np.ascontiguousarray(scaled.reshape(k // 512, 128, 4, n).transpose(0, 1, 3, 2))
    if fmt == "e4m3":
        words = by_word.astype(ml_dtypes.float8_e4m3fn).view(np.uint8)
    else:
        c = by_word.astype(ml_dtypes.float4_e2m1fn).view(np.uint8) & 0xF
        words = c[..., 0::2] | (c[..., 1::2] << 4)
    return np.ascontiguousarray(words), np.ascontiguousarray(byte.astype(np.uint8).reshape(k // 512, 16, n))


def unpack_weight(words, scales, fmt):
    g, p, n, _ = words.shape
    if fmt == "e4m3":
        vals = np.ascontiguousarray(words).view(ml_dtypes.float8_e4m3fn).astype(np.float64)
    else:
        nib = np.empty((g, p, n, 4), np.uint8)
        nib[..., 0::2] = words & 0xF
        nib[..., 1::2] = words >> 4
        vals = E2M1[nib]
    vals = vals * np.repeat(np.exp2(scales.astype(np.float64) - 127.0), 8, axis=1)[..., None]
    return vals.transpose(0, 1, 3, 2).reshape(g * 512, n)

def pack4(w):
    words, scales = pack_weight(w, "e2m1")
    return words.reshape(words.shape[0], 128, -1), scales


def unpack4(words, scales):
    return unpack_weight(words.reshape(words.shape[0], 128, -1, 2), scales, "e2m1")


B, Q, S, D = 4, 256, 512, 1024
K = D + D


def sigmoid(v):
    return 1.0 / (1.0 + np.exp(-v))


def setup_inputs():
    t = mx_kscale(D)
    s = np.concatenate([np.ones(D), t])
    query = bf(np.random.standard_normal((B, Q, D)) * 0.25)
    weighted_ctx = bf(np.random.standard_normal((B, Q, D)) * 0.12 * t)
    W_lin_words, W_lin_scales = pack4(np.random.standard_normal((K, D)) * 5.0 / np.sqrt(K) / s[:, None])
    b_lin = bf(np.random.standard_normal(D) * 0.3)
    W_gate_words, W_gate_scales = pack4(np.random.standard_normal((K, D)) * 5.0 / np.sqrt(K) / s[:, None])
    b_gate = bf(np.random.standard_normal(D) * 0.3)
    return {"query": query,
            "weighted_ctx": weighted_ctx,
            "W_lin_words": W_lin_words,
            "W_lin_scales": W_lin_scales,
            "b_lin": b_lin,
            "W_gate_words": W_gate_words,
            "W_gate_scales": W_gate_scales,
            "b_gate": b_gate}


def reference(query, weighted_ctx, W_lin_words, W_lin_scales, b_lin, W_gate_words, W_gate_scales, b_gate):
    q = f64(query)
    cat = mxq(np.concatenate([q, f64(weighted_ctx)], axis=2), 2, "e4m3")
    h = np.tanh((cat @ unpack4(W_lin_words, W_lin_scales)) + f64(b_lin))
    g = sigmoid((cat @ unpack4(W_gate_words, W_gate_scales)) + f64(b_gate))
    return q * g + h * (1.0 - g)

@@ -1,0 +1,180 @@
+import concourse.mybir as mybir
+from concourse.masks import make_identity
+
+BF16 = mybir.dt.bfloat16
+F32 = mybir.dt.float32
+I32 = mybir.dt.int32
+U32 = mybir.dt.uint32
+U8 = mybir.dt.uint8
+FP8X4 = mybir.dt.float8_e4m3fn_x4
+FP4X4 = mybir.dt.float4_e2m1fn_x4
+ACT = mybir.ActivationFunctionType
+
+P = 128
+PACK = 4
+K_PASS = P * PACK
+TOKENS = 4 * 256
+D = 1024
+K = 2 * D
+PASSES = K // K_PASS
+TILES = TOKENS // P
+N_STEP = 512
+HALVES = D // N_STEP
+STEPS = TILES * HALVES
+WORDS_PER_PASS = K_PASS // 2
+SCALE_ROWS = K_PASS // 32
+
+FLOPS = 2 * TOKENS * K * 2 * D
+
+
+def load_scale_rows(nc, plane, scales):
+    for q in range(SCALE_ROWS // 2):
+        first = 32 * (q // 4) + q % 4
+        nc.sync.dma_start(
+            out=plane[first:P:64, :, :].bitcast(I32),
+            in_=scales[:, q:SCALE_ROWS:8, :].rearrange("g q n -> q g n").bitcast(I32),
+        )
+
+
+def transpose_tokens(nc, xt_pool, grouped, x_tile, ident):
+    x_words = x_tile[:].bitcast(F32)
+    grouped_words = grouped[:].bitcast(F32).rearrange("p (g r u) -> p g r u", g=PASSES, u=2)
+    for bank in range(PASSES // 2):
+        xt = xt_pool.tile([P, 2, 2, P], F32, name="xt")
+        for i in range(2):
+            first = WORDS_PER_PASS * (2 * bank + i)
+            for u in range(2):
+                nc.tensor.transpose(
+                    xt[:, i, u, :], x_words[:, first + u : first + WORDS_PER_PASS : 2], ident[:]
+                )
+        nc.scalar.copy(
+            out=grouped_words[:, 2 * bank : 2 * bank + 2, :, :],
+            in_=xt[:].rearrange("p g u r -> p g r u"),
+        )
+
+
+def mx_group(nc, acc, codes, code_scales, words, plane, n0):
+    for g in range(PASSES):
+        nc.tensor.matmul_mx(
+            out=acc[:],
+            lhsT=codes[:, P * g : P * (g + 1)].bitcast(FP8X4),
+            lhsT_scale=code_scales[:, P * g : P * (g + 1)],
+            rhs=words[g][:, 2 * n0 : 2 * (n0 + N_STEP)].bitcast(FP4X4),
+            rhs_scale=plane[:, g, n0 : n0 + N_STEP],
+            start=(g == 0),
+            stop=(g == PASSES - 1),
+        )
+
+
+def tile_smcmr_pb_kernel(
+    tc, query, weighted_ctx, W_lin_words, W_lin_scales, b_lin, W_gate_words, W_gate_scales, b_gate, out
+):
+    nc = tc.nc
+    query_rows = query.flatten_outer_dims()
+    ctx_rows = weighted_ctx.flatten_outer_dims()
+    out_rows = out.flatten_outer_dims()
+
+    with tc.manual_schedule(), tc.tile_pool(name="keep", bufs=1) as keep, tc.tile_pool(
+        name="quant", bufs=3
+    ) as quant, tc.tile_pool(name="work", bufs=3) as work, tc.psum_pool(
+        name="acc", bufs=3
+    ) as acc_pool, tc.psum_pool(name="xt", bufs=2) as xt_pool:
+        bias_rows = keep.tile([P, 2 * D], BF16)
+        nc.vector.memset(bias_rows[:], 0.0)
+        nc.scalar.dma_start(out=bias_rows[0:1, 0:D], in_=b_lin.unsqueeze(0))
+        nc.scalar.dma_start(out=bias_rows[0:1, D : 2 * D], in_=b_gate.unsqueeze(0))
+        lin_plane = keep.tile([P, PASSES, D], U8, align_bytes=64)
+        gate_plane = keep.tile([P, PASSES, D], U8, align_bytes=64)
+        nc.vector.memset(lin_plane[:].bitcast(I32), 0)
+        nc.vector.memset(gate_plane[:].bitcast(I32), 0)
+        ones = keep.tile([P, P], BF16)
+        nc.vector.memset(ones[:], 1.0)
+        ident = keep.tile([P, P], F32)
+        make_identity(nc, ident[:])
+        warm = keep.tile([P, 1], F32)
+        nc.vector.memset(warm[:], 0.0)
+        nc.scalar.activation(out=warm[:], in_=warm[:], func=ACT.Sigmoid)
+
+        x_tiles = {}
+
+        def load_tokens(m):
+            x_tiles[m] = keep.tile([P, K], BF16, name="x%d" % m)
+            nc.sync.dma_start(out=x_tiles[m][:, 0:D], in_=query_rows[P * m : P * (m + 1), :])
+            nc.sync.dma_start(out=x_tiles[m][:, D:K], in_=ctx_rows[P * m : P * (m + 1), :])
+
+        load_tokens(0)
+        load_tokens(1)
+        load_scale_rows(nc, lin_plane, W_lin_scales)
+        load_scale_rows(nc, gate_plane, W_gate_scales)
+        lin_words = {}
+        gate_words = {}
+        for g in range(PASSES):
+            lin_words[g] = keep.tile([P, 2 * D], U8, align_bytes=64, name="lin_words%d" % g)
+            nc.sync.dma_start(out=lin_words[g][:].bitcast(I32), in_=W_lin_words[g].bitcast(I32))
+        for g in range(PASSES):
+            gate_words[g] = keep.tile([P, 2 * D], U8, align_bytes=64, name="gate_words%d" % g)
+            nc.sync.dma_start(out=gate_words[g][:].bitcast(I32), in_=W_gate_words[g].bitcast(I32))
+        for m in range(2, TILES):
+            load_tokens(m)
+
+        codes = {}
+        code_scales = {}
+
+        def quantise_tokens(m):
+            grouped = quant.tile([P, K], BF16, align_bytes=64, name="grouped")
+            transpose_tokens(nc, xt_pool, grouped, x_tiles[m], ident)
+            codes[m] = quant.tile([P, K // PACK], U32, align_bytes=64, name="codes")
+            code_scales[m] = quant.tile([P, K // PACK], U8, align_bytes=64, name="code_scales")
+            nc.vector.quantize_mx(
+                out=codes[m][:].bitcast(FP8X4), scales=code_scales[m][:], in_=grouped[:]
+            )
+
+        quantise_tokens(0)
+
+        bias = keep.tile([P, 2 * D], F32)
+        for i in range(2 * HALVES):
+            spread = acc_pool.tile([P, N_STEP], F32, name="spread", tag="lin" if i < HALVES else "gate")
+            cols = slice(N_STEP * i, N_STEP * (i + 1))
+            nc.tensor.matmul(out=spread[:], lhsT=ones[:], rhs=bias_rows[:, cols], start=True, stop=True)
+            nc.vector.tensor_copy(out=bias[:, cols], in_=spread[:])
+
+        h = {}
+        gate = {}
+        diff = {}
+        for s in range(STEPS + 1):
+            m, j = divmod(s, HALVES)
+            n0 = N_STEP * j
+            prev_m, prev_j = divmod(s - 1, HALVES)
+            prev_n0 = N_STEP * prev_j
+            multiply = s < STEPS
+            blend = s > 0
+
+            if multiply:
+                if j == 0 and m + 1 < TILES:
+                    quantise_tokens(m + 1)
+                acc_lin = acc_pool.tile([P, N_STEP], F32, name="acc_lin", tag="lin")
+                mx_group(nc, acc_lin, codes[m], code_scales[m], lin_words, lin_plane, n0)
+                acc_gate = acc_pool.tile([P, N_STEP], F32, name="acc_gate", tag="gate")
+                mx_group(nc, acc_gate, codes[m], code_scales[m], gate_words, gate_plane, n0)
+
+            if blend:
+                diff[s - 1] = work.tile([P, N_STEP], F32, name="diff")
+                nc.vector.tensor_sub(
+                    out=diff[s - 1][:], in0=x_tiles[prev_m][:, prev_n0 : prev_n0 + N_STEP], in1=h[s - 1][:]
+                )
+            if multiply:
+                h[s] = work.tile([P, N_STEP], F32, name="h")
+                nc.vector.tensor_add(out=h[s][:], in0=acc_lin[:], in1=bias[:, n0 : n0 + N_STEP])
+                nc.scalar.activation(out=h[s][:], in_=h[s][:], func=ACT.Tanh)
+            if blend:
+                nc.vector.tensor_mul(out=diff[s - 1][:], in0=gate[s - 1][:], in1=diff[s - 1][:])
+            if multiply:
+                gate[s] = work.tile([P, N_STEP], F32, name="gate")
+                nc.vector.tensor_add(out=gate[s][:], in0=acc_gate[:], in1=bias[:, D + n0 : D + n0 + N_STEP])
+                nc.scalar.activation(out=gate[s][:], in_=gate[s][:], func=ACT.Sigmoid)
+            if blend:
+                result = work.tile([P, N_STEP], F32, name="result")
+                nc.vector.tensor_add(out=result[:], in0=diff[s - 1][:], in1=h[s - 1][:])
+                nc.sync.dma_start(
+                    out=out_rows[P * prev_m : P * (prev_m + 1), prev_n0 : prev_n0 + N_STEP], in_=result[:]
+                )

@@ -59,7 +59,7 @@ def mx_group(nc, acc, codes, code_scales, words, plane, n0):
             out=acc[:],
             lhsT=codes[:, P * g : P * (g + 1)].bitcast(FP8X4),
             lhsT_scale=code_scales[:, P * g : P * (g + 1)],
-            rhs=words[g][:, 2 * n0 : 2 * (n0 + N_STEP)].bitcast(FP4X4),
+            rhs=words[:, g, :].bitcast(FP4X4),
             rhs_scale=plane[:, g, n0 : n0 + N_STEP],
             start=(g == 0),
             stop=(g == PASSES - 1),
@@ -102,34 +102,47 @@ def tile_smcmr_pb_kernel(
             nc.sync.dma_start(out=x_tiles[m][:, 0:D], in_=query_rows[P * m : P * (m + 1), :])
             nc.sync.dma_start(out=x_tiles[m][:, D:K], in_=ctx_rows[P * m : P * (m + 1), :])
 
+        lin_words = {}
+        gate_words = {}
+
+        def load_words(words, name, weight, j):
+            words[j] = keep.tile([P, PASSES, 2 * N_STEP], U8, align_bytes=64, name="%s%d" % (name, j))
+            first = 2 * N_STEP * j // 4
+            nc.sync.dma_start(
+                out=words[j][:].bitcast(I32),
+                in_=weight.bitcast(I32)[:, :, first : first + 2 * N_STEP // 4].rearrange("g p w -> p g w"),
+            )
+
         load_tokens(0)
         load_tokens(1)
         load_scale_rows(nc, lin_plane, W_lin_scales)
         load_scale_rows(nc, gate_plane, W_gate_scales)
-        lin_words = {}
-        gate_words = {}
-        for g in range(PASSES):
-            lin_words[g] = keep.tile([P, 2 * D], U8, align_bytes=64, name="lin_words%d" % g)
-            nc.sync.dma_start(out=lin_words[g][:].bitcast(I32), in_=W_lin_words[g].bitcast(I32))
-        for g in range(PASSES):
-            gate_words[g] = keep.tile([P, 2 * D], U8, align_bytes=64, name="gate_words%d" % g)
-            nc.sync.dma_start(out=gate_words[g][:].bitcast(I32), in_=W_gate_words[g].bitcast(I32))
-        for m in range(2, TILES):
+        for j in range(HALVES):
+            load_words(lin_words, "lin_words", W_lin_words, j)
+            load_words(gate_words, "gate_words", W_gate_words, j)
+            load_tokens(2 + j)
+        for m in range(2 + HALVES, TILES):
             load_tokens(m)
 
         codes = {}
         code_scales = {}
 
-        def quantise_tokens(m):
-            grouped = quant.tile([P, K], BF16, align_bytes=64, name="grouped")
-            transpose_tokens(nc, xt_pool, grouped, x_tiles[m], ident)
+        grouped = {}
+
+        def transpose_tile(m):
+            grouped[m] = quant.tile([P, K], BF16, align_bytes=64, name="grouped")
+            transpose_tokens(nc, xt_pool, grouped[m], x_tiles[m], ident)
+
+        def quantise_tile(m):
             codes[m] = quant.tile([P, K // PACK], U32, align_bytes=64, name="codes")
             code_scales[m] = quant.tile([P, K // PACK], U8, align_bytes=64, name="code_scales")
             nc.vector.quantize_mx(
-                out=codes[m][:].bitcast(FP8X4), scales=code_scales[m][:], in_=grouped[:]
+                out=codes[m][:].bitcast(FP8X4), scales=code_scales[m][:], in_=grouped[m][:]
             )
 
-        quantise_tokens(0)
+        transpose_tile(0)
+        quantise_tile(0)
+        transpose_tile(1)
 
         bias = keep.tile([P, 2 * D], F32)
         for i in range(2 * HALVES):
@@ -150,12 +163,14 @@ def tile_smcmr_pb_kernel(
             blend = s > 0
 
             if multiply:
+                if j == 1 and m + 2 < TILES:
+                    transpose_tile(m + 2)
                 if j == 0 and m + 1 < TILES:
-                    quantise_tokens(m + 1)
+                    quantise_tile(m + 1)
                 acc_lin = acc_pool.tile([P, N_STEP], F32, name="acc_lin", tag="lin")
-                mx_group(nc, acc_lin, codes[m], code_scales[m], lin_words, lin_plane, n0)
+                mx_group(nc, acc_lin, codes[m], code_scales[m], lin_words[j], lin_plane, n0)
                 acc_gate = acc_pool.tile([P, N_STEP], F32, name="acc_gate", tag="gate")
-                mx_group(nc, acc_gate, codes[m], code_scales[m], gate_words, gate_plane, n0)
+                mx_group(nc, acc_gate, codes[m], code_scales[m], gate_words[j], gate_plane, n0)
 
             if blend:
                 diff[s - 1] = work.tile([P, N_STEP], F32, name="diff")

@@ -172,15 +172,12 @@ def tile_smcmr_pb_kernel(
                 acc_gate = acc_pool.tile([P, N_STEP], F32, name="acc_gate", tag="gate")
                 mx_group(nc, acc_gate, codes[m], code_scales[m], gate_words[j], gate_plane, n0)
 
-            if blend:
-                diff[s - 1] = work.tile([P, N_STEP], F32, name="diff")
-                nc.vector.tensor_sub(
-                    out=diff[s - 1][:], in0=x_tiles[prev_m][:, prev_n0 : prev_n0 + N_STEP], in1=h[s - 1][:]
-                )
             if multiply:
                 h[s] = work.tile([P, N_STEP], F32, name="h")
                 nc.vector.tensor_add(out=h[s][:], in0=acc_lin[:], in1=bias[:, n0 : n0 + N_STEP])
                 nc.scalar.activation(out=h[s][:], in_=h[s][:], func=ACT.Tanh)
+                diff[s] = work.tile([P, N_STEP], F32, name="diff")
+                nc.gpsimd.tensor_sub(out=diff[s][:], in0=x_tiles[m][:, n0 : n0 + N_STEP], in1=h[s][:])
             if blend:
                 nc.vector.tensor_mul(out=diff[s - 1][:], in0=gate[s - 1][:], in1=diff[s - 1][:])
             if multiply:

@@ -76,7 +76,7 @@ def tile_smcmr_pb_kernel(
 
     with tc.manual_schedule(), tc.tile_pool(name="keep", bufs=1) as keep, tc.tile_pool(
         name="quant", bufs=3
-    ) as quant, tc.tile_pool(name="work", bufs=3) as work, tc.psum_pool(
+    ) as quant, tc.tile_pool(name="work", bufs=4) as work, tc.psum_pool(
         name="acc", bufs=3
     ) as acc_pool, tc.psum_pool(name="xt", bufs=2) as xt_pool:
         bias_rows = keep.tile([P, 2 * D], BF16)
@@ -154,39 +154,42 @@ def tile_smcmr_pb_kernel(
         h = {}
         gate = {}
         diff = {}
-        for s in range(STEPS + 1):
+
+        def start_step(s):
             m, j = divmod(s, HALVES)
             n0 = N_STEP * j
-            prev_m, prev_j = divmod(s - 1, HALVES)
-            prev_n0 = N_STEP * prev_j
-            multiply = s < STEPS
-            blend = s > 0
+            if j == 1 and m + 2 < TILES:
+                transpose_tile(m + 2)
+            acc_lin = acc_pool.tile([P, N_STEP], F32, name="acc_lin", tag="lin")
+            mx_group(nc, acc_lin, codes[m], code_scales[m], lin_words[j], lin_plane, n0)
+            acc_gate = acc_pool.tile([P, N_STEP], F32, name="acc_gate", tag="gate")
+            mx_group(nc, acc_gate, codes[m], code_scales[m], gate_words[j], gate_plane, n0)
 
-            if multiply:
-                if j == 1 and m + 2 < TILES:
-                    transpose_tile(m + 2)
-                if j == 0 and m + 1 < TILES:
-                    quantise_tile(m + 1)
-                acc_lin = acc_pool.tile([P, N_STEP], F32, name="acc_lin", tag="lin")
-                mx_group(nc, acc_lin, codes[m], code_scales[m], lin_words[j], lin_plane, n0)
-                acc_gate = acc_pool.tile([P, N_STEP], F32, name="acc_gate", tag="gate")
-                mx_group(nc, acc_gate, codes[m], code_scales[m], gate_words[j], gate_plane, n0)
+            h[s] = work.tile([P, N_STEP], F32, name="h")
+            nc.vector.tensor_add(out=h[s][:], in0=acc_lin[:], in1=bias[:, n0 : n0 + N_STEP])
+            nc.scalar.activation(out=h[s][:], in_=h[s][:], func=ACT.Tanh)
+            diff[s] = work.tile([P, N_STEP], F32, name="diff")
+            nc.gpsimd.tensor_sub(out=diff[s][:], in0=x_tiles[m][:, n0 : n0 + N_STEP], in1=h[s][:])
+            gate[s] = work.tile([P, N_STEP], F32, name="gate")
+            nc.vector.tensor_add(out=gate[s][:], in0=acc_gate[:], in1=bias[:, D + n0 : D + n0 + N_STEP])
+            nc.scalar.activation(out=gate[s][:], in_=gate[s][:], func=ACT.Sigmoid)
 
-            if multiply:
-                h[s] = work.tile([P, N_STEP], F32, name="h")
-                nc.vector.tensor_add(out=h[s][:], in0=acc_lin[:], in1=bias[:, n0 : n0 + N_STEP])
-                nc.scalar.activation(out=h[s][:], in_=h[s][:], func=ACT.Tanh)
-                diff[s] = work.tile([P, N_STEP], F32, name="diff")
-                nc.gpsimd.tensor_sub(out=diff[s][:], in0=x_tiles[m][:, n0 : n0 + N_STEP], in1=h[s][:])
-            if blend:
-                nc.vector.tensor_mul(out=diff[s - 1][:], in0=gate[s - 1][:], in1=diff[s - 1][:])
-            if multiply:
-                gate[s] = work.tile([P, N_STEP], F32, name="gate")
-                nc.vector.tensor_add(out=gate[s][:], in0=acc_gate[:], in1=bias[:, D + n0 : D + n0 + N_STEP])
-                nc.scalar.activation(out=gate[s][:], in_=gate[s][:], func=ACT.Sigmoid)
-            if blend:
-                result = work.tile([P, N_STEP], F32, name="result")
-                nc.vector.tensor_add(out=result[:], in0=diff[s - 1][:], in1=h[s - 1][:])
-                nc.sync.dma_start(
-                    out=out_rows[P * prev_m : P * (prev_m + 1), prev_n0 : prev_n0 + N_STEP], in_=result[:]
-                )
+        def scale_by_gate(s):
+            nc.vector.tensor_mul(out=diff[s][:], in0=gate[s][:], in1=diff[s][:])
+
+        def finish_step(s):
+            m, j = divmod(s, HALVES)
+            n0 = N_STEP * j
+            result = work.tile([P, N_STEP], F32, name="result")
+            nc.vector.tensor_add(out=result[:], in0=diff[s][:], in1=h[s][:])
+            nc.sync.dma_start(out=out_rows[P * m : P * (m + 1), n0 : n0 + N_STEP], in_=result[:])
+
+        for s in range(STEPS + 2):
+            if s < STEPS:
+                start_step(s)
+            if 1 <= s <= STEPS:
+                scale_by_gate(s - 1)
+            if s >= 2:
+                finish_step(s - 2)
+            if s % HALVES == 0 and s // HALVES + 1 < TILES:
+                quantise_tile(s // HALVES + 1)

@@ -23,44 +23,45 @@ HALVES = D // N_STEP
 STEPS = TILES * HALVES
 WORDS_PER_PASS = K_PASS // 2
 SCALE_ROWS = K_PASS // 32
+SOURCES = 2
+PASSES_PER_SOURCE = PASSES // SOURCES
 
 FLOPS = 2 * TOKENS * K * 2 * D
 
 
-def load_scale_rows(nc, plane, scales):
-    for q in range(SCALE_ROWS // 2):
-        first = 32 * (q // 4) + q % 4
+def load_scale_rows(nc, plane, scales, n0):
+    for r in range(4):
         nc.sync.dma_start(
-            out=plane[first:P:64, :, :].bitcast(I32),
-            in_=scales[:, q:SCALE_ROWS:8, :].rearrange("g q n -> q g n").bitcast(I32),
+            out=plane[r:P:32, :, :].bitcast(I32),
+            in_=scales[:, r:SCALE_ROWS:4, n0 : n0 + N_STEP].rearrange("g q n -> q g n").bitcast(I32),
         )
 
 
-def transpose_tokens(nc, xt_pool, grouped, x_tile, ident):
+def transpose_source(nc, xt_pool, grouped, x_tile, ident, source):
     x_words = x_tile[:].bitcast(F32)
     grouped_words = grouped[:].bitcast(F32).rearrange("p (g r u) -> p g r u", g=PASSES, u=2)
-    for bank in range(PASSES // 2):
-        xt = xt_pool.tile([P, 2, 2, P], F32, name="xt")
-        for i in range(2):
-            first = WORDS_PER_PASS * (2 * bank + i)
-            for u in range(2):
-                nc.tensor.transpose(
-                    xt[:, i, u, :], x_words[:, first + u : first + WORDS_PER_PASS : 2], ident[:]
-                )
-        nc.scalar.copy(
-            out=grouped_words[:, 2 * bank : 2 * bank + 2, :, :],
-            in_=xt[:].rearrange("p g u r -> p g r u"),
-        )
+    g0 = PASSES_PER_SOURCE * source
+    xt = xt_pool.tile([P, PASSES_PER_SOURCE, 2, P], F32, name="xt")
+    for i in range(PASSES_PER_SOURCE):
+        first = WORDS_PER_PASS * (g0 + i)
+        for u in range(2):
+            nc.tensor.transpose(
+                xt[:, i, u, :], x_words[:, first + u : first + WORDS_PER_PASS : 2], ident[:]
+            )
+    nc.scalar.copy(
+        out=grouped_words[:, g0 : g0 + PASSES_PER_SOURCE, :, :],
+        in_=xt[:].rearrange("p g u r -> p g r u"),
+    )
 
 
-def mx_group(nc, acc, codes, code_scales, words, plane, n0):
+def mx_group(nc, acc, codes, code_scales, words, plane):
     for g in range(PASSES):
         nc.tensor.matmul_mx(
             out=acc[:],
             lhsT=codes[:, P * g : P * (g + 1)].bitcast(FP8X4),
             lhsT_scale=code_scales[:, P * g : P * (g + 1)],
             rhs=words[:, g, :].bitcast(FP4X4),
-            rhs_scale=plane[:, g, n0 : n0 + N_STEP],
+            rhs_scale=plane[:, g, :],
             start=(g == 0),
             stop=(g == PASSES - 1),
         )
@@ -75,31 +76,39 @@ def tile_smcmr_pb_kernel(
     out_rows = out.flatten_outer_dims()
 
     with tc.manual_schedule(), tc.tile_pool(name="keep", bufs=1) as keep, tc.tile_pool(
-        name="quant", bufs=3
+        name="quant", bufs=4
     ) as quant, tc.tile_pool(name="work", bufs=4) as work, tc.psum_pool(
         name="acc", bufs=3
     ) as acc_pool, tc.psum_pool(name="xt", bufs=2) as xt_pool:
-        bias_rows = keep.tile([P, 2 * D], BF16)
+        bias_rows = keep.tile([P, N_STEP], BF16)
         nc.vector.memset(bias_rows[:], 0.0)
-        nc.scalar.dma_start(out=bias_rows[0:1, 0:D], in_=b_lin.unsqueeze(0))
-        nc.scalar.dma_start(out=bias_rows[0:1, D : 2 * D], in_=b_gate.unsqueeze(0))
-        lin_plane = keep.tile([P, PASSES, D], U8, align_bytes=64)
-        gate_plane = keep.tile([P, PASSES, D], U8, align_bytes=64)
-        nc.vector.memset(lin_plane[:].bitcast(I32), 0)
-        nc.vector.memset(gate_plane[:].bitcast(I32), 0)
-        ones = keep.tile([P, P], BF16)
-        nc.vector.memset(ones[:], 1.0)
+        nc.scalar.dma_start(out=bias_rows[0:HALVES, :], in_=b_lin.rearrange("(j n) -> j n", n=N_STEP))
+        nc.scalar.dma_start(
+            out=bias_rows[HALVES : 2 * HALVES, :], in_=b_gate.rearrange("(j n) -> j n", n=N_STEP)
+        )
+        warm = keep.tile([P, 1], F32)
+        nc.gpsimd.memset(warm[:], 0.0)
+        nc.scalar.activation(out=warm[:], in_=warm[:], func=ACT.Sigmoid)
+        lin_plane = {}
+        gate_plane = {}
+        for j in range(HALVES):
+            lin_plane[j] = keep.tile([P, PASSES, N_STEP], U8, align_bytes=64, name="lin_plane%d" % j)
+            nc.vector.memset(lin_plane[j][:].bitcast(I32), 0)
+            gate_plane[j] = keep.tile([P, PASSES, N_STEP], U8, align_bytes=64, name="gate_plane%d" % j)
+            nc.vector.memset(gate_plane[j][:].bitcast(I32), 0)
         ident = keep.tile([P, P], F32)
         make_identity(nc, ident[:])
-        warm = keep.tile([P, 1], F32)
-        nc.vector.memset(warm[:], 0.0)
-        nc.scalar.activation(out=warm[:], in_=warm[:], func=ACT.Sigmoid)
+        ident_bf = keep.tile([P, P], BF16)
+        make_identity(nc, ident_bf[:])
 
         x_tiles = {}
-
-        def load_tokens(m):
+        for m in range(TILES):
             x_tiles[m] = keep.tile([P, K], BF16, name="x%d" % m)
+
+        def load_query(m):
             nc.sync.dma_start(out=x_tiles[m][:, 0:D], in_=query_rows[P * m : P * (m + 1), :])
+
+        def load_ctx(m):
             nc.sync.dma_start(out=x_tiles[m][:, D:K], in_=ctx_rows[P * m : P * (m + 1), :])
 
         lin_words = {}
@@ -113,83 +122,128 @@ def tile_smcmr_pb_kernel(
                 in_=weight.bitcast(I32)[:, :, first : first + 2 * N_STEP // 4].rearrange("g p w -> p g w"),
             )
 
-        load_tokens(0)
-        load_tokens(1)
-        load_scale_rows(nc, lin_plane, W_lin_scales)
-        load_scale_rows(nc, gate_plane, W_gate_scales)
-        for j in range(HALVES):
-            load_words(lin_words, "lin_words", W_lin_words, j)
-            load_words(gate_words, "gate_words", W_gate_words, j)
-            load_tokens(2 + j)
-        for m in range(2 + HALVES, TILES):
-            load_tokens(m)
+        load_query(0)
+        load_scale_rows(nc, lin_plane[0], W_lin_scales, 0)
+        load_words(lin_words, "lin_words", W_lin_words, 0)
+        load_ctx(0)
+        load_query(1)
+        load_ctx(1)
+        load_scale_rows(nc, gate_plane[0], W_gate_scales, 0)
+        load_words(gate_words, "gate_words", W_gate_words, 0)
+        load_scale_rows(nc, lin_plane[1], W_lin_scales, N_STEP)
+        load_scale_rows(nc, gate_plane[1], W_gate_scales, N_STEP)
+        load_words(lin_words, "lin_words", W_lin_words, 1)
+        load_words(gate_words, "gate_words", W_gate_words, 1)
+        for m in range(2, TILES):
+            load_query(m)
+            load_ctx(m)
 
         codes = {}
         code_scales = {}
-
         grouped = {}
 
-        def transpose_tile(m):
+        def open_tile(m):
             grouped[m] = quant.tile([P, K], BF16, align_bytes=64, name="grouped")
-            transpose_tokens(nc, xt_pool, grouped[m], x_tiles[m], ident)
-
-        def quantise_tile(m):
             codes[m] = quant.tile([P, K // PACK], U32, align_bytes=64, name="codes")
             code_scales[m] = quant.tile([P, K // PACK], U8, align_bytes=64, name="code_scales")
+
+        def transpose_half(m, source):
+            transpose_source(nc, xt_pool, grouped[m], x_tiles[m], ident, source)
+
+        def quantise(m, first, width):
+            words = slice(first // PACK, (first + width) // PACK)
             nc.vector.quantize_mx(
-                out=codes[m][:].bitcast(FP8X4), scales=code_scales[m][:], in_=grouped[m][:]
+                out=codes[m][:, words].bitcast(FP8X4),
+                scales=code_scales[m][:, words],
+                in_=grouped[m][:, first : first + width],
             )
 
-        transpose_tile(0)
-        quantise_tile(0)
-        transpose_tile(1)
-
         bias = keep.tile([P, 2 * D], F32)
-        for i in range(2 * HALVES):
-            spread = acc_pool.tile([P, N_STEP], F32, name="spread", tag="lin" if i < HALVES else "gate")
-            cols = slice(N_STEP * i, N_STEP * (i + 1))
-            nc.tensor.matmul(out=spread[:], lhsT=ones[:], rhs=bias_rows[:, cols], start=True, stop=True)
-            nc.vector.tensor_copy(out=bias[:, cols], in_=spread[:])
 
+        def spread_bias(row, copy):
+            spread = acc_pool.tile([P, N_STEP], F32, name="spread", tag="lin" if row < HALVES else "gate")
+            nc.tensor.matmul(
+                out=spread[:],
+                lhsT=ident_bf[:, row : row + 1].to_broadcast([P, P]),
+                rhs=bias_rows[:],
+                start=True,
+                stop=True,
+            )
+            copy(out=bias[:, N_STEP * row : N_STEP * (row + 1)], in_=spread[:])
+
+        order = [(pair + i, j) for pair in range(0, TILES, 2) for j in range(HALVES) for i in range(2)]
         h = {}
         gate = {}
         diff = {}
+        acc_lin = {}
+        acc_gate = {}
 
-        def start_step(s):
-            m, j = divmod(s, HALVES)
+        def multiply_lin(s):
+            m, j = order[s]
+            acc_lin[s] = acc_pool.tile([P, N_STEP], F32, name="acc_lin", tag="lin")
+            mx_group(nc, acc_lin[s], codes[m], code_scales[m], lin_words[j], lin_plane[j])
+
+        def multiply_gate(s):
+            m, j = order[s]
+            acc_gate[s] = acc_pool.tile([P, N_STEP], F32, name="acc_gate", tag="gate")
+            mx_group(nc, acc_gate[s], codes[m], code_scales[m], gate_words[j], gate_plane[j])
+
+        def activate_lin(s):
+            m, j = order[s]
             n0 = N_STEP * j
-            if j == 1 and m + 2 < TILES:
-                transpose_tile(m + 2)
-            acc_lin = acc_pool.tile([P, N_STEP], F32, name="acc_lin", tag="lin")
-            mx_group(nc, acc_lin, codes[m], code_scales[m], lin_words[j], lin_plane, n0)
-            acc_gate = acc_pool.tile([P, N_STEP], F32, name="acc_gate", tag="gate")
-            mx_group(nc, acc_gate, codes[m], code_scales[m], gate_words[j], gate_plane, n0)
-
             h[s] = work.tile([P, N_STEP], F32, name="h")
-            nc.vector.tensor_add(out=h[s][:], in0=acc_lin[:], in1=bias[:, n0 : n0 + N_STEP])
+            nc.vector.tensor_add(out=h[s][:], in0=acc_lin[s][:], in1=bias[:, n0 : n0 + N_STEP])
             nc.scalar.activation(out=h[s][:], in_=h[s][:], func=ACT.Tanh)
             diff[s] = work.tile([P, N_STEP], F32, name="diff")
             nc.gpsimd.tensor_sub(out=diff[s][:], in0=x_tiles[m][:, n0 : n0 + N_STEP], in1=h[s][:])
+
+        def activate_gate(s):
+            n0 = N_STEP * order[s][1]
             gate[s] = work.tile([P, N_STEP], F32, name="gate")
-            nc.vector.tensor_add(out=gate[s][:], in0=acc_gate[:], in1=bias[:, D + n0 : D + n0 + N_STEP])
+            nc.vector.tensor_add(out=gate[s][:], in0=acc_gate[s][:], in1=bias[:, D + n0 : D + n0 + N_STEP])
             nc.scalar.activation(out=gate[s][:], in_=gate[s][:], func=ACT.Sigmoid)
 
         def scale_by_gate(s):
             nc.vector.tensor_mul(out=diff[s][:], in0=gate[s][:], in1=diff[s][:])
 
         def finish_step(s):
-            m, j = divmod(s, HALVES)
+            m, j = order[s]
             n0 = N_STEP * j
             result = work.tile([P, N_STEP], F32, name="result")
             nc.vector.tensor_add(out=result[:], in0=diff[s][:], in1=h[s][:])
             nc.sync.dma_start(out=out_rows[P * m : P * (m + 1), n0 : n0 + N_STEP], in_=result[:])
 
+        open_tile(0)
+        transpose_half(0, 0)
+        quantise(0, 0, D)
+        spread_bias(0, nc.vector.tensor_copy)
+        spread_bias(HALVES, nc.vector.tensor_copy)
+        transpose_half(0, 1)
+        quantise(0, D, D)
+        spread_bias(1, nc.scalar.copy)
+        spread_bias(HALVES + 1, nc.scalar.copy)
+
         for s in range(STEPS + 2):
+            ahead = order[s + 2] if s + 2 < STEPS else None
+            fresh = ahead is not None and ahead[1] == 0 and ahead[0] >= 2
+            if fresh:
+                open_tile(ahead[0])
+                transpose_half(ahead[0], 0)
+                transpose_half(ahead[0], 1)
             if s < STEPS:
-                start_step(s)
+                multiply_lin(s)
+                if s == 0:
+                    open_tile(1)
+                    transpose_half(1, 0)
+                    transpose_half(1, 1)
+                multiply_gate(s)
+                activate_lin(s)
+                if s == 0:
+                    quantise(1, 0, K)
+                activate_gate(s)
             if 1 <= s <= STEPS:
                 scale_by_gate(s - 1)
             if s >= 2:
                 finish_step(s - 2)
-            if s % HALVES == 0 and s // HALVES + 1 < TILES:
-                quantise_tile(s // HALVES + 1)
+            if fresh:
+                quantise(ahead[0], 0, K)

@@ -37,8 +37,7 @@ def load_scale_rows(nc, plane, scales, n0):
         )
 
 
-def transpose_source(nc, xt_pool, grouped, x_tile, ident, source):
-    x_words = x_tile[:].bitcast(F32)
+def transpose_source(nc, xt_pool, grouped, x_words, step, column, ident, source):
     grouped_words = grouped[:].bitcast(F32).rearrange("p (g r u) -> p g r u", g=PASSES, u=2)
     g0 = PASSES_PER_SOURCE * source
     xt = xt_pool.tile([P, PASSES_PER_SOURCE, 2, P], F32, name="xt")
@@ -46,7 +45,7 @@ def transpose_source(nc, xt_pool, grouped, x_tile, ident, source):
         first = WORDS_PER_PASS * (g0 + i)
         for u in range(2):
             nc.tensor.transpose(
-                xt[:, i, u, :], x_words[:, first + u : first + WORDS_PER_PASS : 2], ident[:]
+                xt[:, i, u, :], x_words[:, first + column * u : first + column * u + step * (P - 1) + 1 : step], ident[:]
             )
     nc.scalar.copy(
         out=grouped_words[:, g0 : g0 + PASSES_PER_SOURCE, :, :],
@@ -78,10 +77,10 @@ def tile_smcmr_pb_kernel(
     with tc.manual_schedule(), tc.tile_pool(name="keep", bufs=1) as keep, tc.tile_pool(
         name="quant", bufs=4
     ) as quant, tc.tile_pool(name="work", bufs=4) as work, tc.psum_pool(
-        name="acc", bufs=3
+        name="acc", bufs=6
     ) as acc_pool, tc.psum_pool(name="xt", bufs=2) as xt_pool:
         bias_rows = keep.tile([P, N_STEP], BF16)
-        nc.vector.memset(bias_rows[:], 0.0)
+        nc.vector.memset(bias_rows[:].bitcast(I32), 0)
         nc.scalar.dma_start(out=bias_rows[0:HALVES, :], in_=b_lin.rearrange("(j n) -> j n", n=N_STEP))
         nc.scalar.dma_start(
             out=bias_rows[HALVES : 2 * HALVES, :], in_=b_gate.rearrange("(j n) -> j n", n=N_STEP)
@@ -123,13 +122,13 @@ def tile_smcmr_pb_kernel(
             )
 
         load_query(0)
+        load_ctx(0)
         load_scale_rows(nc, lin_plane[0], W_lin_scales, 0)
         load_words(lin_words, "lin_words", W_lin_words, 0)
-        load_ctx(0)
-        load_query(1)
-        load_ctx(1)
         load_scale_rows(nc, gate_plane[0], W_gate_scales, 0)
         load_words(gate_words, "gate_words", W_gate_words, 0)
+        load_query(1)
+        load_ctx(1)
         load_scale_rows(nc, lin_plane[1], W_lin_scales, N_STEP)
         load_scale_rows(nc, gate_plane[1], W_gate_scales, N_STEP)
         load_words(lin_words, "lin_words", W_lin_words, 1)
@@ -141,14 +140,28 @@ def tile_smcmr_pb_kernel(
         codes = {}
         code_scales = {}
         grouped = {}
+        gathered = {}
 
         def open_tile(m):
             grouped[m] = quant.tile([P, K], BF16, align_bytes=64, name="grouped")
             codes[m] = quant.tile([P, K // PACK], U32, align_bytes=64, name="codes")
             code_scales[m] = quant.tile([P, K // PACK], U8, align_bytes=64, name="code_scales")
 
+        def gather_words(m):
+            gathered[m] = quant.tile([P, K // 2], F32, name="gathered")
+            for source in range(SOURCES):
+                words = slice(D // 2 * source, D // 2 * (source + 1))
+                nc.scalar.copy(
+                    out=gathered[m][:, words].rearrange("p (g u r) -> p g u r", u=2, r=P),
+                    in_=x_tiles[m][:].bitcast(F32)[:, words].rearrange("p (g r u) -> p g u r", u=2, r=P),
+                )
+
         def transpose_half(m, source):
-            transpose_source(nc, xt_pool, grouped[m], x_tiles[m], ident, source)
+            if m in gathered:
+                words, step, column = gathered[m], 1, P
+            else:
+                words, step, column = x_tiles[m][:].bitcast(F32), 2, 1
+            transpose_source(nc, xt_pool, grouped[m], words, step, column, ident, source)
 
         def quantise(m, first, width):
             words = slice(first // PACK, (first + width) // PACK)
@@ -161,7 +174,7 @@ def tile_smcmr_pb_kernel(
         bias = keep.tile([P, 2 * D], F32)
 
         def spread_bias(row, copy):
-            spread = acc_pool.tile([P, N_STEP], F32, name="spread", tag="lin" if row < HALVES else "gate")
+            spread = acc_pool.tile([P, N_STEP], F32, name="spread", tag="acc")
             nc.tensor.matmul(
                 out=spread[:],
                 lhsT=ident_bf[:, row : row + 1].to_broadcast([P, P]),
@@ -171,7 +184,8 @@ def tile_smcmr_pb_kernel(
             )
             copy(out=bias[:, N_STEP * row : N_STEP * (row + 1)], in_=spread[:])
 
-        order = [(pair + i, j) for pair in range(0, TILES, 2) for j in range(HALVES) for i in range(2)]
+        order = [(i, j) for j in range(HALVES) for i in range(2)]
+        order += [(m, j) for m in range(2, TILES) for j in range(HALVES)]
         h = {}
         gate = {}
         diff = {}
@@ -180,12 +194,12 @@ def tile_smcmr_pb_kernel(
 
         def multiply_lin(s):
             m, j = order[s]
-            acc_lin[s] = acc_pool.tile([P, N_STEP], F32, name="acc_lin", tag="lin")
+            acc_lin[s] = acc_pool.tile([P, N_STEP], F32, name="acc_lin", tag="acc")
             mx_group(nc, acc_lin[s], codes[m], code_scales[m], lin_words[j], lin_plane[j])
 
         def multiply_gate(s):
             m, j = order[s]
-            acc_gate[s] = acc_pool.tile([P, N_STEP], F32, name="acc_gate", tag="gate")
+            acc_gate[s] = acc_pool.tile([P, N_STEP], F32, name="acc_gate", tag="acc")
             mx_group(nc, acc_gate[s], codes[m], code_scales[m], gate_words[j], gate_plane[j])
 
         def activate_lin(s):
@@ -194,6 +208,10 @@ def tile_smcmr_pb_kernel(
             h[s] = work.tile([P, N_STEP], F32, name="h")
             nc.vector.tensor_add(out=h[s][:], in0=acc_lin[s][:], in1=bias[:, n0 : n0 + N_STEP])
             nc.scalar.activation(out=h[s][:], in_=h[s][:], func=ACT.Tanh)
+
+        def subtract(s):
+            m, j = order[s]
+            n0 = N_STEP * j
             diff[s] = work.tile([P, N_STEP], F32, name="diff")
             nc.gpsimd.tensor_sub(out=diff[s][:], in0=x_tiles[m][:, n0 : n0 + N_STEP], in1=h[s][:])
 
@@ -223,27 +241,40 @@ def tile_smcmr_pb_kernel(
         spread_bias(1, nc.scalar.copy)
         spread_bias(HALVES + 1, nc.scalar.copy)
 
-        for s in range(STEPS + 2):
-            ahead = order[s + 2] if s + 2 < STEPS else None
-            fresh = ahead is not None and ahead[1] == 0 and ahead[0] >= 2
-            if fresh:
-                open_tile(ahead[0])
-                transpose_half(ahead[0], 0)
-                transpose_half(ahead[0], 1)
+        first_step = {}
+        for s, (m, j) in enumerate(order):
+            first_step.setdefault(m, s)
+        tile_from = {s: m for m, s in first_step.items()}
+
+        multiply_lin(0)
+        open_tile(1)
+        transpose_half(1, 0)
+        transpose_half(1, 1)
+        multiply_gate(0)
+        activate_lin(0)
+        subtract(0)
+        quantise(1, 0, K)
+        activate_gate(0)
+
+        for s in range(1, STEPS + 2):
+            fresh = tile_from.get(s + 2)
+            later = tile_from.get(s + 4)
             if s < STEPS:
                 multiply_lin(s)
-                if s == 0:
-                    open_tile(1)
-                    transpose_half(1, 0)
-                    transpose_half(1, 1)
-                multiply_gate(s)
+                if fresh is not None:
+                    open_tile(fresh)
+                    transpose_half(fresh, 0)
+                    transpose_half(fresh, 1)
                 activate_lin(s)
-                if s == 0:
-                    quantise(1, 0, K)
-                activate_gate(s)
-            if 1 <= s <= STEPS:
-                scale_by_gate(s - 1)
+                subtract(s)
+                multiply_gate(s)
             if s >= 2:
                 finish_step(s - 2)
-            if fresh:
-                quantise(ahead[0], 0, K)
+            if s <= STEPS:
+                scale_by_gate(s - 1)
+            if fresh is not None:
+                quantise(fresh, 0, K)
+            if later is not None:
+                gather_words(later)
+            if s < STEPS:
+                activate_gate(s)

@@ -113,27 +113,33 @@ def tile_smcmr_pb_kernel(
         lin_words = {}
         gate_words = {}
 
-        def load_words(words, name, weight, j):
+        def load_words(words, name, weight, j, parts=1):
             words[j] = keep.tile([P, PASSES, 2 * N_STEP], U8, align_bytes=64, name="%s%d" % (name, j))
             first = 2 * N_STEP * j // 4
-            nc.sync.dma_start(
-                out=words[j][:].bitcast(I32),
-                in_=weight.bitcast(I32)[:, :, first : first + 2 * N_STEP // 4].rearrange("g p w -> p g w"),
-            )
+            for i in range(parts):
+                passes = slice(PASSES * i // parts, PASSES * (i + 1) // parts)
+                nc.sync.dma_start(
+                    out=words[j][:, passes, :].bitcast(I32),
+                    in_=weight.bitcast(I32)[passes, :, first : first + 2 * N_STEP // 4].rearrange(
+                        "g p w -> p g w"
+                    ),
+                )
 
         load_query(0)
         load_ctx(0)
         load_scale_rows(nc, lin_plane[0], W_lin_scales, 0)
         load_words(lin_words, "lin_words", W_lin_words, 0)
-        load_scale_rows(nc, gate_plane[0], W_gate_scales, 0)
-        load_words(gate_words, "gate_words", W_gate_words, 0)
         load_query(1)
         load_ctx(1)
+        load_scale_rows(nc, gate_plane[0], W_gate_scales, 0)
+        load_words(gate_words, "gate_words", W_gate_words, 0, parts=2)
+        load_query(2)
+        load_ctx(2)
         load_scale_rows(nc, lin_plane[1], W_lin_scales, N_STEP)
-        load_scale_rows(nc, gate_plane[1], W_gate_scales, N_STEP)
         load_words(lin_words, "lin_words", W_lin_words, 1)
+        load_scale_rows(nc, gate_plane[1], W_gate_scales, N_STEP)
         load_words(gate_words, "gate_words", W_gate_words, 1)
-        for m in range(2, TILES):
+        for m in range(3, TILES):
             load_query(m)
             load_ctx(m)
 
@@ -215,21 +221,38 @@ def tile_smcmr_pb_kernel(
             diff[s] = work.tile([P, N_STEP], F32, name="diff")
             nc.gpsimd.tensor_sub(out=diff[s][:], in0=x_tiles[m][:, n0 : n0 + N_STEP], in1=h[s][:])
 
-        def activate_gate(s):
-            n0 = N_STEP * order[s][1]
+        WHOLE = [slice(0, N_STEP)]
+        PARTS = [slice(0, N_STEP // 2), slice(N_STEP // 2, N_STEP)]
+
+        def activate_gate(s, parts=WHOLE):
+            n0 = D + N_STEP * order[s][1]
             gate[s] = work.tile([P, N_STEP], F32, name="gate")
-            nc.vector.tensor_add(out=gate[s][:], in0=acc_gate[s][:], in1=bias[:, D + n0 : D + n0 + N_STEP])
-            nc.scalar.activation(out=gate[s][:], in_=gate[s][:], func=ACT.Sigmoid)
+            for part in parts:
+                nc.vector.tensor_add(
+                    out=gate[s][:, part],
+                    in0=acc_gate[s][:, part],
+                    in1=bias[:, n0 + part.start : n0 + part.stop],
+                )
+                nc.scalar.activation(out=gate[s][:, part], in_=gate[s][:, part], func=ACT.Sigmoid)
 
-        def scale_by_gate(s):
-            nc.vector.tensor_mul(out=diff[s][:], in0=gate[s][:], in1=diff[s][:])
+        def scale_by_gate(s, parts=WHOLE):
+            for part in parts:
+                nc.vector.tensor_mul(
+                    out=diff[s][:, part], in0=gate[s][:, part], in1=diff[s][:, part]
+                )
 
-        def finish_step(s):
+        def finish_step(s, parts=WHOLE):
             m, j = order[s]
             n0 = N_STEP * j
             result = work.tile([P, N_STEP], F32, name="result")
-            nc.vector.tensor_add(out=result[:], in0=diff[s][:], in1=h[s][:])
-            nc.sync.dma_start(out=out_rows[P * m : P * (m + 1), n0 : n0 + N_STEP], in_=result[:])
+            for part in parts:
+                nc.vector.tensor_add(
+                    out=result[:, part], in0=diff[s][:, part], in1=h[s][:, part]
+                )
+                nc.sync.dma_start(
+                    out=out_rows[P * m : P * (m + 1), n0 + part.start : n0 + part.stop],
+                    in_=result[:, part],
+                )
 
         open_tile(0)
         transpose_half(0, 0)
@@ -253,28 +276,30 @@ def tile_smcmr_pb_kernel(
         multiply_gate(0)
         activate_lin(0)
         subtract(0)
-        quantise(1, 0, K)
+        for source in range(SOURCES):
+            quantise(1, D * source, D)
         activate_gate(0)
 
-        for s in range(1, STEPS + 2):
+        for s in range(1, STEPS):
             fresh = tile_from.get(s + 2)
             later = tile_from.get(s + 4)
-            if s < STEPS:
-                multiply_lin(s)
-                if fresh is not None:
-                    open_tile(fresh)
-                    transpose_half(fresh, 0)
-                    transpose_half(fresh, 1)
-                activate_lin(s)
-                subtract(s)
-                multiply_gate(s)
+            multiply_lin(s)
+            if fresh is not None:
+                open_tile(fresh)
+                transpose_half(fresh, 0)
+                transpose_half(fresh, 1)
+            activate_lin(s)
+            subtract(s)
+            multiply_gate(s)
             if s >= 2:
                 finish_step(s - 2)
-            if s <= STEPS:
-                scale_by_gate(s - 1)
+            scale_by_gate(s - 1)
             if fresh is not None:
                 quantise(fresh, 0, K)
             if later is not None:
                 gather_words(later)
-            if s < STEPS:
-                activate_gate(s)
+            activate_gate(s, PARTS if s == STEPS - 1 else WHOLE)
+
+        finish_step(STEPS - 2)
+        scale_by_gate(STEPS - 1, PARTS)
+        finish_step(STEPS - 1, PARTS)

import concourse.mybir as mybir
from concourse.masks import make_identity

BF16 = mybir.dt.bfloat16
F32 = mybir.dt.float32
I32 = mybir.dt.int32
U32 = mybir.dt.uint32
U8 = mybir.dt.uint8
FP8X4 = mybir.dt.float8_e4m3fn_x4
FP4X4 = mybir.dt.float4_e2m1fn_x4
ACT = mybir.ActivationFunctionType

P = 128
PACK = 4
K_PASS = P * PACK
TOKENS = 4 * 256
D = 1024
K = 2 * D
PASSES = K // K_PASS
TILES = TOKENS // P
N_STEP = 512
HALVES = D // N_STEP
STEPS = TILES * HALVES
WORDS_PER_PASS = K_PASS // 2
SCALE_ROWS = K_PASS // 32
SOURCES = 2
PASSES_PER_SOURCE = PASSES // SOURCES

FLOPS = 2 * TOKENS * K * 2 * D


def load_scale_rows(nc, plane, scales, n0):
    for r in range(4):
        nc.sync.dma_start(
            out=plane[r:P:32, :, :].bitcast(I32),
            in_=scales[:, r:SCALE_ROWS:4, n0 : n0 + N_STEP].rearrange("g q n -> q g n").bitcast(I32),
        )


def transpose_source(nc, xt_pool, grouped, x_words, step, column, ident, source):
    grouped_words = grouped[:].bitcast(F32).rearrange("p (g r u) -> p g r u", g=PASSES, u=2)
    g0 = PASSES_PER_SOURCE * source
    xt = xt_pool.tile([P, PASSES_PER_SOURCE, 2, P], F32, name="xt")
    for i in range(PASSES_PER_SOURCE):
        first = WORDS_PER_PASS * (g0 + i)
        for u in range(2):
            nc.tensor.transpose(
                xt[:, i, u, :], x_words[:, first + column * u : first + column * u + step * (P - 1) + 1 : step], ident[:]
            )
    nc.scalar.copy(
        out=grouped_words[:, g0 : g0 + PASSES_PER_SOURCE, :, :],
        in_=xt[:].rearrange("p g u r -> p g r u"),
    )


def mx_group(nc, acc, codes, code_scales, words, plane):
    for g in range(PASSES):
        nc.tensor.matmul_mx(
            out=acc[:],
            lhsT=codes[:, P * g : P * (g + 1)].bitcast(FP8X4),
            lhsT_scale=code_scales[:, P * g : P * (g + 1)],
            rhs=words[:, g, :].bitcast(FP4X4),
            rhs_scale=plane[:, g, :],
            start=(g == 0),
            stop=(g == PASSES - 1),
        )


def tile_smcmr_pb_kernel(
    tc, query, weighted_ctx, W_lin_words, W_lin_scales, b_lin, W_gate_words, W_gate_scales, b_gate, out
):
    nc = tc.nc
    query_rows = query.flatten_outer_dims()
    ctx_rows = weighted_ctx.flatten_outer_dims()
    out_rows = out.flatten_outer_dims()

    with tc.manual_schedule(), tc.tile_pool(name="keep", bufs=1) as keep, tc.tile_pool(
        name="quant", bufs=4
    ) as quant, tc.tile_pool(name="work", bufs=4) as work, tc.psum_pool(
        name="acc", bufs=6
    ) as acc_pool, tc.psum_pool(name="xt", bufs=2) as xt_pool:
        bias_rows = keep.tile([P, N_STEP], BF16)
        nc.vector.memset(bias_rows[:].bitcast(I32), 0)
        nc.scalar.dma_start(out=bias_rows[0:HALVES, :], in_=b_lin.rearrange("(j n) -> j n", n=N_STEP))
        nc.scalar.dma_start(
            out=bias_rows[HALVES : 2 * HALVES, :], in_=b_gate.rearrange("(j n) -> j n", n=N_STEP)
        )
        warm = keep.tile([P, 1], F32)
        nc.gpsimd.memset(warm[:], 0.0)
        nc.scalar.activation(out=warm[:], in_=warm[:], func=ACT.Sigmoid)
        lin_plane = {}
        gate_plane = {}
        for j in range(HALVES):
            lin_plane[j] = keep.tile([P, PASSES, N_STEP], U8, align_bytes=64, name="lin_plane%d" % j)
            nc.vector.memset(lin_plane[j][:].bitcast(I32), 0)
            gate_plane[j] = keep.tile([P, PASSES, N_STEP], U8, align_bytes=64, name="gate_plane%d" % j)
            nc.vector.memset(gate_plane[j][:].bitcast(I32), 0)
        ident = keep.tile([P, P], F32)
        make_identity(nc, ident[:])
        ident_bf = keep.tile([P, P], BF16)
        make_identity(nc, ident_bf[:])

        x_tiles = {}
        for m in range(TILES):
            x_tiles[m] = keep.tile([P, K], BF16, name="x%d" % m)

        def load_query(m):
            nc.sync.dma_start(out=x_tiles[m][:, 0:D], in_=query_rows[P * m : P * (m + 1), :])

        def load_ctx(m):
            nc.sync.dma_start(out=x_tiles[m][:, D:K], in_=ctx_rows[P * m : P * (m + 1), :])

        lin_words = {}
        gate_words = {}

        def load_words(words, name, weight, j, parts=1):
            words[j] = keep.tile([P, PASSES, 2 * N_STEP], U8, align_bytes=64, name="%s%d" % (name, j))
            first = 2 * N_STEP * j // 4
            for i in range(parts):
                passes = slice(PASSES * i // parts, PASSES * (i + 1) // parts)
                nc.sync.dma_start(
                    out=words[j][:, passes, :].bitcast(I32),
                    in_=weight.bitcast(I32)[passes, :, first : first + 2 * N_STEP // 4].rearrange(
                        "g p w -> p g w"
                    ),
                )

        load_query(0)
        load_ctx(0)
        load_scale_rows(nc, lin_plane[0], W_lin_scales, 0)
        load_words(lin_words, "lin_words", W_lin_words, 0)
        load_query(1)
        load_ctx(1)
        load_scale_rows(nc, gate_plane[0], W_gate_scales, 0)
        load_words(gate_words, "gate_words", W_gate_words, 0, parts=2)
        load_query(2)
        load_ctx(2)
        load_scale_rows(nc, lin_plane[1], W_lin_scales, N_STEP)
        load_words(lin_words, "lin_words", W_lin_words, 1)
        load_scale_rows(nc, gate_plane[1], W_gate_scales, N_STEP)
        load_words(gate_words, "gate_words", W_gate_words, 1)
        for m in range(3, TILES):
            load_query(m)
            load_ctx(m)

        codes = {}
        code_scales = {}
        grouped = {}
        gathered = {}

        def open_tile(m):
            grouped[m] = quant.tile([P, K], BF16, align_bytes=64, name="grouped")
            codes[m] = quant.tile([P, K // PACK], U32, align_bytes=64, name="codes")
            code_scales[m] = quant.tile([P, K // PACK], U8, align_bytes=64, name="code_scales")

        def gather_words(m):
            gathered[m] = quant.tile([P, K // 2], F32, name="gathered")
            for source in range(SOURCES):
                words = slice(D // 2 * source, D // 2 * (source + 1))
                nc.scalar.copy(
                    out=gathered[m][:, words].rearrange("p (g u r) -> p g u r", u=2, r=P),
                    in_=x_tiles[m][:].bitcast(F32)[:, words].rearrange("p (g r u) -> p g u r", u=2, r=P),
                )

        def transpose_half(m, source):
            if m in gathered:
                words, step, column = gathered[m], 1, P
            else:
                words, step, column = x_tiles[m][:].bitcast(F32), 2, 1
            transpose_source(nc, xt_pool, grouped[m], words, step, column, ident, source)

        def quantise(m, first, width):
            words = slice(first // PACK, (first + width) // PACK)
            nc.vector.quantize_mx(
                out=codes[m][:, words].bitcast(FP8X4),
                scales=code_scales[m][:, words],
                in_=grouped[m][:, first : first + width],
            )

        bias = keep.tile([P, 2 * D], F32)

        def spread_bias(row, copy):
            spread = acc_pool.tile([P, N_STEP], F32, name="spread", tag="acc")
            nc.tensor.matmul(
                out=spread[:],
                lhsT=ident_bf[:, row : row + 1].to_broadcast([P, P]),
                rhs=bias_rows[:],
                start=True,
                stop=True,
            )
            copy(out=bias[:, N_STEP * row : N_STEP * (row + 1)], in_=spread[:])

        order = [(i, j) for j in range(HALVES) for i in range(2)]
        order += [(m, j) for m in range(2, TILES) for j in range(HALVES)]
        h = {}
        gate = {}
        diff = {}
        acc_lin = {}
        acc_gate = {}

        def multiply_lin(s):
            m, j = order[s]
            acc_lin[s] = acc_pool.tile([P, N_STEP], F32, name="acc_lin", tag="acc")
            mx_group(nc, acc_lin[s], codes[m], code_scales[m], lin_words[j], lin_plane[j])

        def multiply_gate(s):
            m, j = order[s]
            acc_gate[s] = acc_pool.tile([P, N_STEP], F32, name="acc_gate", tag="acc")
            mx_group(nc, acc_gate[s], codes[m], code_scales[m], gate_words[j], gate_plane[j])

        def activate_lin(s):
            m, j = order[s]
            n0 = N_STEP * j
            h[s] = work.tile([P, N_STEP], F32, name="h")
            nc.vector.tensor_add(out=h[s][:], in0=acc_lin[s][:], in1=bias[:, n0 : n0 + N_STEP])
            nc.scalar.activation(out=h[s][:], in_=h[s][:], func=ACT.Tanh)

        def subtract(s):
            m, j = order[s]
            n0 = N_STEP * j
            diff[s] = work.tile([P, N_STEP], F32, name="diff")
            nc.gpsimd.tensor_sub(out=diff[s][:], in0=x_tiles[m][:, n0 : n0 + N_STEP], in1=h[s][:])

        WHOLE = [slice(0, N_STEP)]
        PARTS = [slice(0, N_STEP // 2), slice(N_STEP // 2, N_STEP)]

        def activate_gate(s, parts=WHOLE):
            n0 = D + N_STEP * order[s][1]
            gate[s] = work.tile([P, N_STEP], F32, name="gate")
            for part in parts:
                nc.vector.tensor_add(
                    out=gate[s][:, part],
                    in0=acc_gate[s][:, part],
                    in1=bias[:, n0 + part.start : n0 + part.stop],
                )
                nc.scalar.activation(out=gate[s][:, part], in_=gate[s][:, part], func=ACT.Sigmoid)

        def scale_by_gate(s, parts=WHOLE):
            for part in parts:
                nc.vector.tensor_mul(
                    out=diff[s][:, part], in0=gate[s][:, part], in1=diff[s][:, part]
                )

        def finish_step(s, parts=WHOLE):
            m, j = order[s]
            n0 = N_STEP * j
            result = work.tile([P, N_STEP], F32, name="result")
            for part in parts:
                nc.vector.tensor_add(
                    out=result[:, part], in0=diff[s][:, part], in1=h[s][:, part]
                )
                nc.sync.dma_start(
                    out=out_rows[P * m : P * (m + 1), n0 + part.start : n0 + part.stop],
                    in_=result[:, part],
                )

        open_tile(0)
        transpose_half(0, 0)
        quantise(0, 0, D)
        spread_bias(0, nc.vector.tensor_copy)
        spread_bias(HALVES, nc.vector.tensor_copy)
        transpose_half(0, 1)
        quantise(0, D, D)
        spread_bias(1, nc.scalar.copy)
        spread_bias(HALVES + 1, nc.scalar.copy)

        first_step = {}
        for s, (m, j) in enumerate(order):
            first_step.setdefault(m, s)
        tile_from = {s: m for m, s in first_step.items()}

        multiply_lin(0)
        open_tile(1)
        transpose_half(1, 0)
        transpose_half(1, 1)
        multiply_gate(0)
        activate_lin(0)
        subtract(0)
        for source in range(SOURCES):
            quantise(1, D * source, D)
        activate_gate(0)

        for s in range(1, STEPS):
            fresh = tile_from.get(s + 2)
            later = tile_from.get(s + 4)
            multiply_lin(s)
            if fresh is not None:
                open_tile(fresh)
                transpose_half(fresh, 0)
                transpose_half(fresh, 1)
            activate_lin(s)
            subtract(s)
            multiply_gate(s)
            if s >= 2:
                finish_step(s - 2)
            scale_by_gate(s - 1)
            if fresh is not None:
                quantise(fresh, 0, K)
            if later is not None:
                gather_words(later)
            activate_gate(s, PARTS if s == STEPS - 1 else WHOLE)

        finish_step(STEPS - 2)
        scale_by_gate(STEPS - 1, PARTS)
        finish_step(STEPS - 1, PARTS)
